import numpy as np
import ml_dtypes


def mxq(x, axis, fmt="e4m3"):
    dtype, down = {"e4m3": (ml_dtypes.float8_e4m3fn, 7), "e5m2": (ml_dtypes.float8_e5m2, 14)}[fmt]
    v = np.moveaxis(np.asarray(x, np.float32).astype(ml_dtypes.bfloat16).astype(np.float64), axis, -1)
    blocks = v.reshape(v.shape[:-1] + (-1, 32))
    amax = np.abs(blocks).max(-1, keepdims=True)
    byte = np.maximum(np.where(amax > 0, np.frexp(amax)[1] - 1 + 127, 0) - down, 1)
    scale = np.exp2(byte - 127.0)
    codes = (blocks / scale).astype(np.float32).astype(dtype).astype(np.float64)
    return np.moveaxis((codes * scale).reshape(v.shape), -1, axis)


WIDE = False


def mx_kscale(k):
    if not WIDE:
        return np.ones(k)
    levels = np.array([10, -10, 5, -5, 0])
    a = np.random.permutation(np.resize(levels, k // 512 * 4)).reshape(k // 512, 4)
    idx = np.arange(k)
    return np.exp2(a[idx // 512, idx % 128 // 32])


BF16 = ml_dtypes.bfloat16


def bf(x):
    return np.asarray(x, np.float32).astype(BF16)


def f64(x):
    return np.asarray(x).astype(np.float64)


E2M1 = np.array([0.0, 0.5, 1.0, 1.5, 2.0, 3.0, 4.0, 6.0, -0.0, -0.5, -1.0, -1.5, -2.0, -3.0, -4.0, -6.0])


def pack_weight(w, fmt):
    k, n = w.shape
    w = f64(bf(w)).reshape(k // 32, 32, n)
    amax = np.abs(w).max(1)
    if fmt == "e4m3":
        byte = np.frexp(amax)[1] - 1 + 127 - 7
    else:
        mant, ex = np.frexp(amax / 6.0)
        byte = np.where(mant > 0.5, ex, ex - 1) + 127
    byte = np.clip(np.where(amax > 0, byte, 1), 1, 254)
    scaled = (w * np.exp2(127.0 - byte)[:, None, :]).reshape(k, n).astype(np.float32)
    by_word = np.ascontiguousarray(scaled.reshape(k // 512, 128, 4, n).transpose(0, 1, 3, 2))
    if fmt == "e4m3":
        words = by_word.astype(ml_dtypes.float8_e4m3fn).view(np.uint8)
    else:
        c = by_word.astype(ml_dtypes.float4_e2m1fn).view(np.uint8) & 0xF
        words = c[..., 0::2] | (c[..., 1::2] << 4)
    return np.ascontiguousarray(words), np.ascontiguousarray(byte.astype(np.uint8).reshape(k // 512, 16, n))


def unpack_weight(words, scales, fmt):
    g, p, n, _ = words.shape
    if fmt == "e4m3":
        vals = np.ascontiguousarray(words).view(ml_dtypes.float8_e4m3fn).astype(np.float64)
    else:
        nib = np.empty((g, p, n, 4), np.uint8)
        nib[..., 0::2] = words & 0xF
        nib[..., 1::2] = words >> 4
        vals = E2M1[nib]
    vals = vals * np.repeat(np.exp2(scales.astype(np.float64) - 127.0), 8, axis=1)[..., None]
    return vals.transpose(0, 1, 3, 2).reshape(g * 512, n)

def pack4(w):
    words, scales = pack_weight(w, "e2m1")
    return words.reshape(words.shape[0], 128, -1), scales


def unpack4(words, scales):
    return unpack_weight(words.reshape(words.shape[0], 128, -1, 2), scales, "e2m1")


B, HH, WW, C, NH, DIM = 2, 16, 32, 512, 8, 128
N = HH * WW
HD = NH * DIM
F = 4 * HD
BN_EPS = 1e-5
WS = 0.02
GQK = np.sqrt(2.8) / DIM ** 0.25
GV = 4.0


def heads(t):
    return t.reshape(B, N, NH, DIM).transpose(0, 2, 1, 3)


def setup_inputs():
    s = mx_kscale(C)
    x = np.random.standard_normal((B, HH, WW, C)) + 0.5 * np.random.standard_normal(C)
    gain = np.concatenate([np.full(2 * HD, GQK), np.full(2 * HD, GV)])
    inputs = bf(x * s)
    words, scales = pack4(np.random.standard_normal((C, F)) * WS / np.sqrt(C) / s[:, None])
    return {"inputs": inputs,
            "w_qkv_words": words,
            "w_qkv_scales": scales,
            "bn_scale": bf(np.random.standard_normal(F) * gain)}


def reference(inputs, w_qkv_words, w_qkv_scales, bn_scale):
    x = mxq(f64(inputs).reshape(B * N, C), 1, "e4m3") @ unpack4(w_qkv_words, w_qkv_scales)
    mean = x.mean(axis=0)
    var = x.var(axis=0)
    x = (x - mean) / np.sqrt(var + BN_EPS) * f64(bn_scale)
    q, k, v1, v2 = (heads(t) for t in np.split(x.reshape(B, N, F), 4, axis=-1))
    v = np.concatenate((v1, v2), axis=-1)
    return np.ascontiguousarray(q), np.ascontiguousarray(k), v

@@ -1,0 +1,205 @@
+from contextlib import ExitStack
+
+import concourse.mybir as mybir
+from concourse.masks import make_identity
+
+F32 = mybir.dt.float32
+BF16 = mybir.dt.bfloat16
+I32 = mybir.dt.int32
+U32 = mybir.dt.uint32
+U8 = mybir.dt.uint8
+FP8X4 = mybir.dt.float8_e4m3fn_x4
+FP4X4 = mybir.dt.float4_e2m1fn_x4
+ALU = mybir.AluOpType
+ACT = mybir.ActivationFunctionType
+
+P = 128
+PACK = 4
+MAPS = 2
+PIXELS = 512
+CHANNELS = 512
+COLUMNS = 4096
+HEADS = 8
+DIM = 128
+BLOCKS = PIXELS // P
+TILES = COLUMNS // P
+BN_EPS = 1e-5
+STATS = 6
+
+FLOPS = 2 * MAPS * PIXELS * CHANNELS * COLUMNS
+
+
+def tile_levitattention_pa_kernel(
+    tc, inputs, w_qkv_words, w_qkv_scales, bn_scale, out_0, out_1, out_2
+):
+    nc = tc.nc
+
+    stores = []
+    for h in range(HEADS):
+        stores.append((out_0[:, h], [h]))
+    for h in range(HEADS):
+        stores.append((out_1[:, h], [HEADS + h]))
+    for h in range(HEADS):
+        stores.append((out_2[:, h], [2 * HEADS + h, 3 * HEADS + h]))
+    work = []
+    for n, (dest, tiles) in enumerate(stores):
+        for part, c in enumerate(tiles):
+            work.append((c, n, part))
+
+    with ExitStack() as ctx:
+        keep = ctx.enter_context(tc.tile_pool(name="keep", bufs=1))
+        small = ctx.enter_context(tc.tile_pool(name="small", bufs=4))
+        normal = ctx.enter_context(tc.tile_pool(name="normal", bufs=3))
+        result = ctx.enter_context(tc.tile_pool(name="result", bufs=3))
+        psum = ctx.enter_context(tc.psum_pool(name="psum", bufs=1))
+        ctx.enter_context(tc.manual_schedule())
+
+        x_sb = keep.tile([P, MAPS, BLOCKS, CHANNELS], BF16)
+        x_rows = inputs.rearrange("b h w c -> b (h w) c")
+        for b in range(MAPS):
+            nc.sync.dma_start(
+                out=x_sb[:, b].rearrange("p t c -> p (t c)"),
+                in_=x_rows[b].rearrange("(p t) c -> p (t c)", t=BLOCKS),
+            )
+
+        w_plane = keep.tile([P, COLUMNS], U8, align_bytes=64)
+        nc.vector.memset(w_plane[:].bitcast(I32), 0)
+        for quadrant in range(4):
+            nc.sync.dma_start(
+                out=w_plane[32 * quadrant : 32 * quadrant + 4, :].bitcast(I32),
+                in_=w_qkv_scales[0, 4 * quadrant : 4 * quadrant + 4, :].bitcast(I32),
+            )
+
+        w_words = keep.tile([P, 2 * COLUMNS], U8, align_bytes=64)
+        quarter = 2 * COLUMNS // 4
+        for j in range(4):
+            nc.sync.dma_start(
+                out=w_words[:, j * quarter : (j + 1) * quarter].bitcast(I32),
+                in_=w_qkv_words[0, :, j * quarter : (j + 1) * quarter].bitcast(I32),
+            )
+
+        gain_rows = keep.tile([P, P], BF16)
+        nc.vector.memset(gain_rows[:], 0.0)
+        nc.scalar.dma_start(out=gain_rows[0:TILES, :], in_=bn_scale.rearrange("(i f) -> i f", f=P))
+
+        identity = keep.tile([P, P], F32)
+        make_identity(nc, identity[:])
+        minus_half = keep.tile([P, 1], F32)
+        nc.gpsimd.memset(minus_half[:], -0.5)
+
+        x_codes = keep.tile([P, MAPS, PIXELS], U32, align_bytes=64)
+        x_plane = keep.tile([P, MAPS, PIXELS], U8, align_bytes=64)
+        for b in range(MAPS):
+            grouped = keep.tile([P, PIXELS, PACK], BF16, align_bytes=64, name="grouped%d" % b)
+            for pair in range(BLOCKS // 2):
+                flipped = psum.tile([P, 2, 2, P], F32, tag="product", bufs=6)
+                for j in range(2):
+                    words = x_sb[:, b, 2 * pair + j, :].bitcast(F32)
+                    for u in range(2):
+                        nc.tensor.transpose(flipped[:, j, u, :], words[:, u : CHANNELS // 2 : 2], identity[:])
+                pixels = slice(2 * pair * P, 2 * (pair + 1) * P)
+                side_by_side = grouped[:, pixels, :].bitcast(F32).rearrange("p (j r) u -> p j r u", j=2)
+                if pair == 0:
+                    nc.vector.tensor_copy(out=side_by_side, in_=flipped[:].rearrange("p j u r -> p j r u"))
+                else:
+                    nc.scalar.copy(out=side_by_side, in_=flipped[:].rearrange("p j u r -> p j r u"))
+            nc.vector.quantize_mx(
+                out=x_codes[:, b, :].bitcast(FP8X4),
+                scales=x_plane[:, b, :],
+                in_=grouped[:].rearrange("p r t -> p (r t)"),
+            )
+
+        gain_wide = keep.tile([P, P], F32)
+        nc.vector.tensor_copy(out=gain_wide[:], in_=gain_rows[:])
+        gain_flipped = psum.tile([P, P], F32, tag="flipped", bufs=2)
+        nc.tensor.transpose(gain_flipped[:], gain_wide[:], identity[:])
+        gain = keep.tile([P, TILES], F32)
+        nc.vector.tensor_copy(out=gain[:], in_=gain_flipped[:, 0:TILES])
+
+        products = {}
+        moments = {}
+        factors = {}
+        normals = {}
+        flips = {}
+        results = {}
+
+        def project(i):
+            c = work[i][0]
+            products[i] = []
+            for b in range(MAPS):
+                product = psum.tile([P, PIXELS], F32, tag="product", bufs=6)
+                nc.tensor.matmul_mx(
+                    out=product[:],
+                    lhsT=w_words[:, 2 * c * P : 2 * (c + 1) * P].bitcast(FP4X4),
+                    lhsT_scale=w_plane[:, c * P : (c + 1) * P],
+                    rhs=x_codes[:, b, :].bitcast(FP8X4),
+                    rhs_scale=x_plane[:, b, :],
+                    start=True,
+                    stop=True,
+                )
+                products[i].append(product)
+
+        def statistics(i):
+            c = work[i][0]
+            partial = small.tile([P, MAPS, STATS], F32)
+            for b in range(MAPS):
+                nc.vector.bn_stats(out=partial[:, b, :], in_=products[i][b][:])
+            mean_var = small.tile([P, 2], F32)
+            nc.vector.bn_aggr(out=mean_var[:], in_=partial[:].rearrange("p b s -> p (b s)"))
+            factor = small.tile([P, 4], F32)
+            nc.gpsimd.tensor_scalar(
+                out=factor[:, 0:1], in0=mean_var[:, 1:2], scalar1=BN_EPS, scalar2=1.0, op0=ALU.add, op1=ALU.mult
+            )
+            nc.gpsimd.tensor_tensor(out=factor[:, 1:2], in0=factor[:, 0:1], in1=minus_half[:], op=ALU.pow)
+            nc.gpsimd.tensor_tensor(out=factor[:, 2:3], in0=factor[:, 1:2], in1=gain[:, c : c + 1], op=ALU.mult)
+            nc.gpsimd.tensor_scalar(
+                out=factor[:, 3:4], in0=mean_var[:, 0:1], scalar1=factor[:, 2:3], scalar2=-1.0,
+                op0=ALU.mult, op1=ALU.mult,
+            )
+            moments[i] = mean_var
+            factors[i] = factor
+
+        def normalise(i):
+            normalised = normal.tile([P, MAPS, PIXELS], F32)
+            nc.scalar.activation(
+                out=normalised[:, 0, :], in_=products[i][0][:], func=ACT.Identity,
+                scale=factors[i][:, 2:3], bias=factors[i][:, 3:4],
+            )
+            nc.vector.tensor_scalar(
+                out=normalised[:, 1, :], in0=products[i][1][:], scalar1=moments[i][:, 0:1],
+                scalar2=factors[i][:, 2:3], op0=ALU.subtract, op1=ALU.mult,
+            )
+            normals[i] = normalised
+
+        def flip(i):
+            flips[i] = []
+            for b in range(MAPS):
+                flipped = psum.tile([P, BLOCKS, DIM], F32, tag="flipped", bufs=2)
+                for t in range(BLOCKS):
+                    nc.tensor.transpose(flipped[:, t, :], normals[i][:, b, t * P : (t + 1) * P], identity[:])
+                flips[i].append(flipped)
+
+        def store(i):
+            c, n, part = work[i]
+            dest, tiles = stores[n]
+            if part == 0:
+                results[n] = result.tile([P, MAPS, BLOCKS, len(tiles), DIM], F32, name="head", tag="head")
+            for b in range(MAPS):
+                nc.scalar.copy(out=results[n][:, b, :, part, :], in_=flips[i][b][:])
+            if part == len(tiles) - 1:
+                nc.sync.dma_start(
+                    out=dest.rearrange("b (p t) e -> p b (t e)", t=BLOCKS),
+                    in_=results[n][:].rearrange("p b t g d -> p b (t g d)"),
+                )
+
+        for step in range(-1, TILES + 3):
+            if 0 <= step - 2 < TILES:
+                normalise(step - 2)
+            if 0 <= step + 1 < TILES:
+                project(step + 1)
+            if 0 <= step - 3 < TILES:
+                store(step - 3)
+            if 0 <= step - 2 < TILES:
+                flip(step - 2)
+            if 0 <= step + 1 < TILES:
+                statistics(step + 1)

@@ -92,7 +92,7 @@ def tile_levitattention_pa_kernel(
         for b in range(MAPS):
             grouped = keep.tile([P, PIXELS, PACK], BF16, align_bytes=64, name="grouped%d" % b)
             for pair in range(BLOCKS // 2):
-                flipped = psum.tile([P, 2, 2, P], F32, tag="product", bufs=6)
+                flipped = psum.tile([P, 2, 2, P], F32, tag="bank", bufs=8)
                 for j in range(2):
                     words = x_sb[:, b, 2 * pair + j, :].bitcast(F32)
                     for u in range(2):
@@ -111,13 +111,12 @@ def tile_levitattention_pa_kernel(
 
         gain_wide = keep.tile([P, P], F32)
         nc.vector.tensor_copy(out=gain_wide[:], in_=gain_rows[:])
-        gain_flipped = psum.tile([P, P], F32, tag="flipped", bufs=2)
+        gain_flipped = psum.tile([P, P], F32, tag="bank", bufs=8)
         nc.tensor.transpose(gain_flipped[:], gain_wide[:], identity[:])
         gain = keep.tile([P, TILES], F32)
         nc.vector.tensor_copy(out=gain[:], in_=gain_flipped[:, 0:TILES])
 
         products = {}
-        moments = {}
         factors = {}
         normals = {}
         flips = {}
@@ -127,7 +126,7 @@ def tile_levitattention_pa_kernel(
             c = work[i][0]
             products[i] = []
             for b in range(MAPS):
-                product = psum.tile([P, PIXELS], F32, tag="product", bufs=6)
+                product = psum.tile([P, PIXELS], F32, tag="bank", bufs=8)
                 nc.tensor.matmul_mx(
                     out=product[:],
                     lhsT=w_words[:, 2 * c * P : 2 * (c + 1) * P].bitcast(FP4X4),
@@ -156,25 +155,21 @@ def tile_levitattention_pa_kernel(
                 out=factor[:, 3:4], in0=mean_var[:, 0:1], scalar1=factor[:, 2:3], scalar2=-1.0,
                 op0=ALU.mult, op1=ALU.mult,
             )
-            moments[i] = mean_var
             factors[i] = factor
 
         def normalise(i):
             normalised = normal.tile([P, MAPS, PIXELS], F32)
-            nc.scalar.activation(
-                out=normalised[:, 0, :], in_=products[i][0][:], func=ACT.Identity,
-                scale=factors[i][:, 2:3], bias=factors[i][:, 3:4],
-            )
-            nc.vector.tensor_scalar(
-                out=normalised[:, 1, :], in0=products[i][1][:], scalar1=moments[i][:, 0:1],
-                scalar2=factors[i][:, 2:3], op0=ALU.subtract, op1=ALU.mult,
-            )
+            for b in range(MAPS):
+                nc.scalar.activation(
+                    out=normalised[:, b, :], in_=products[i][b][:], func=ACT.Identity,
+                    scale=factors[i][:, 2:3], bias=factors[i][:, 3:4],
+                )
             normals[i] = normalised
 
         def flip(i):
             flips[i] = []
             for b in range(MAPS):
-                flipped = psum.tile([P, BLOCKS, DIM], F32, tag="flipped", bufs=2)
+                flipped = psum.tile([P, BLOCKS, DIM], F32, tag="bank", bufs=8)
                 for t in range(BLOCKS):
                     nc.tensor.transpose(flipped[:, t, :], normals[i][:, b, t * P : (t + 1) * P], identity[:])
                 flips[i].append(flipped)
@@ -184,8 +179,8 @@ def tile_levitattention_pa_kernel(
             dest, tiles = stores[n]
             if part == 0:
                 results[n] = result.tile([P, MAPS, BLOCKS, len(tiles), DIM], F32, name="head", tag="head")
-            for b in range(MAPS):
-                nc.scalar.copy(out=results[n][:, b, :, part, :], in_=flips[i][b][:])
+            nc.scalar.copy(out=results[n][:, 0, :, part, :], in_=flips[i][0][:])
+            nc.vector.tensor_copy(out=results[n][:, 1, :, part, :], in_=flips[i][1][:])
             if part == len(tiles) - 1:
                 nc.sync.dma_start(
                     out=dest.rearrange("b (p t) e -> p b (t e)", t=BLOCKS),

@@ -36,11 +36,11 @@ def tile_levitattention_pa_kernel(
 
     stores = []
     for h in range(HEADS):
+        stores.append((out_2[:, h], [2 * HEADS + h, 3 * HEADS + h]))
+    for h in range(HEADS):
         stores.append((out_0[:, h], [h]))
     for h in range(HEADS):
         stores.append((out_1[:, h], [HEADS + h]))
-    for h in range(HEADS):
-        stores.append((out_2[:, h], [2 * HEADS + h, 3 * HEADS + h]))
     work = []
     for n, (dest, tiles) in enumerate(stores):
         for part, c in enumerate(tiles):
@@ -48,19 +48,20 @@ def tile_levitattention_pa_kernel(
 
     with ExitStack() as ctx:
         keep = ctx.enter_context(tc.tile_pool(name="keep", bufs=1))
-        small = ctx.enter_context(tc.tile_pool(name="small", bufs=4))
-        normal = ctx.enter_context(tc.tile_pool(name="normal", bufs=3))
-        result = ctx.enter_context(tc.tile_pool(name="result", bufs=3))
+        small = ctx.enter_context(tc.tile_pool(name="small", bufs=6))
+        normal = ctx.enter_context(tc.tile_pool(name="normal", bufs=4))
+        result = ctx.enter_context(tc.tile_pool(name="result", bufs=4))
         psum = ctx.enter_context(tc.psum_pool(name="psum", bufs=1))
         ctx.enter_context(tc.manual_schedule())
 
         x_sb = keep.tile([P, MAPS, BLOCKS, CHANNELS], BF16)
         x_rows = inputs.rearrange("b h w c -> b (h w) c")
         for b in range(MAPS):
-            nc.sync.dma_start(
-                out=x_sb[:, b].rearrange("p t c -> p (t c)"),
-                in_=x_rows[b].rearrange("(p t) c -> p (t c)", t=BLOCKS),
-            )
+            x_map = x_rows[b].rearrange("(p t) c -> p t c", t=BLOCKS)
+            for pair in range(BLOCKS // 2):
+                nc.sync.dma_start(
+                    out=x_sb[:, b, 2 * pair : 2 * pair + 2, :], in_=x_map[:, 2 * pair : 2 * pair + 2, :]
+                )
 
         w_plane = keep.tile([P, COLUMNS], U8, align_bytes=64)
         nc.vector.memset(w_plane[:].bitcast(I32), 0)
@@ -72,7 +73,7 @@ def tile_levitattention_pa_kernel(
 
         w_words = keep.tile([P, 2 * COLUMNS], U8, align_bytes=64)
         quarter = 2 * COLUMNS // 4
-        for j in range(4):
+        for j in (2, 3, 0, 1):
             nc.sync.dma_start(
                 out=w_words[:, j * quarter : (j + 1) * quarter].bitcast(I32),
                 in_=w_qkv_words[0, :, j * quarter : (j + 1) * quarter].bitcast(I32),
@@ -103,11 +104,11 @@ def tile_levitattention_pa_kernel(
                     nc.vector.tensor_copy(out=side_by_side, in_=flipped[:].rearrange("p j u r -> p j r u"))
                 else:
                     nc.scalar.copy(out=side_by_side, in_=flipped[:].rearrange("p j u r -> p j r u"))
-            nc.vector.quantize_mx(
-                out=x_codes[:, b, :].bitcast(FP8X4),
-                scales=x_plane[:, b, :],
-                in_=grouped[:].rearrange("p r t -> p (r t)"),
-            )
+                nc.vector.quantize_mx(
+                    out=x_codes[:, b, pixels].bitcast(FP8X4),
+                    scales=x_plane[:, b, pixels],
+                    in_=grouped[:, pixels, :].rearrange("p r t -> p (r t)"),
+                )
 
         gain_wide = keep.tile([P, P], F32)
         nc.vector.tensor_copy(out=gain_wide[:], in_=gain_rows[:])

@@ -85,8 +85,6 @@ def tile_levitattention_pa_kernel(
 
         identity = keep.tile([P, P], F32)
         make_identity(nc, identity[:])
-        minus_half = keep.tile([P, 1], F32)
-        nc.gpsimd.memset(minus_half[:], -0.5)
 
         x_codes = keep.tile([P, MAPS, PIXELS], U32, align_bytes=64)
         x_plane = keep.tile([P, MAPS, PIXELS], U8, align_bytes=64)
@@ -114,11 +112,15 @@ def tile_levitattention_pa_kernel(
         nc.vector.tensor_copy(out=gain_wide[:], in_=gain_rows[:])
         gain_flipped = psum.tile([P, P], F32, tag="bank", bufs=8)
         nc.tensor.transpose(gain_flipped[:], gain_wide[:], identity[:])
-        gain = keep.tile([P, TILES], F32)
-        nc.vector.tensor_copy(out=gain[:], in_=gain_flipped[:, 0:TILES])
+        gain_pair = keep.tile([P, TILES, 2], F32)
+        nc.vector.tensor_copy(out=gain_pair[:, :, 0], in_=gain_flipped[:, 0:TILES])
+        nc.vector.tensor_scalar(
+            out=gain_pair[:, :, 1], in0=gain_flipped[:, 0:TILES], scalar1=-1.0, scalar2=0.0, op0=ALU.mult, op1=ALU.add
+        )
 
         products = {}
         factors = {}
+        means = {}
         normals = {}
         flips = {}
         results = {}
@@ -146,15 +148,21 @@ def tile_levitattention_pa_kernel(
                 nc.vector.bn_stats(out=partial[:, b, :], in_=products[i][b][:])
             mean_var = small.tile([P, 2], F32)
             nc.vector.bn_aggr(out=mean_var[:], in_=partial[:].rearrange("p b s -> p (b s)"))
+            means[i] = mean_var
+
+        def chain(i):
+            c = work[i][0]
             factor = small.tile([P, 4], F32)
-            nc.gpsimd.tensor_scalar(
-                out=factor[:, 0:1], in0=mean_var[:, 1:2], scalar1=BN_EPS, scalar2=1.0, op0=ALU.add, op1=ALU.mult
+            nc.scalar.activation(
+                out=factor[:, 0:1], in_=means[i][:, 1:2], func=ACT.Abs_reciprocal_sqrt, bias=BN_EPS, scale=1.0
             )
-            nc.gpsimd.tensor_tensor(out=factor[:, 1:2], in0=factor[:, 0:1], in1=minus_half[:], op=ALU.pow)
-            nc.gpsimd.tensor_tensor(out=factor[:, 2:3], in0=factor[:, 1:2], in1=gain[:, c : c + 1], op=ALU.mult)
             nc.gpsimd.tensor_scalar(
-                out=factor[:, 3:4], in0=mean_var[:, 0:1], scalar1=factor[:, 2:3], scalar2=-1.0,
-                op0=ALU.mult, op1=ALU.mult,
+                out=factor[:, 2:4], in0=gain_pair[:, c, :], scalar1=factor[:, 0:1], scalar2=0.0,
+                op0=ALU.mult, op1=ALU.add,
+            )
+            nc.gpsimd.tensor_scalar(
+                out=factor[:, 1:2], in0=means[i][:, 0:1], scalar1=factor[:, 3:4], scalar2=0.0,
+                op0=ALU.mult, op1=ALU.add,
             )
             factors[i] = factor
 
@@ -163,7 +171,7 @@ def tile_levitattention_pa_kernel(
             for b in range(MAPS):
                 nc.scalar.activation(
                     out=normalised[:, b, :], in_=products[i][b][:], func=ACT.Identity,
-                    scale=factors[i][:, 2:3], bias=factors[i][:, 3:4],
+                    scale=factors[i][:, 2:3], bias=factors[i][:, 1:2],
                 )
             normals[i] = normalised
 
@@ -195,6 +203,8 @@ def tile_levitattention_pa_kernel(
                 project(step + 1)
             if 0 <= step - 3 < TILES:
                 store(step - 3)
+            if 0 <= step < TILES:
+                chain(step)
             if 0 <= step - 2 < TILES:
                 flip(step - 2)
             if 0 <= step + 1 < TILES:

@@ -54,6 +54,11 @@ def tile_levitattention_pa_kernel(
         psum = ctx.enter_context(tc.psum_pool(name="psum", bufs=1))
         ctx.enter_context(tc.manual_schedule())
 
+        one = keep.tile([P, 1], F32)
+        nc.gpsimd.memset(one[:], 1.0)
+        warm = keep.tile([P, 1], F32)
+        nc.scalar.activation(out=warm[:], in_=one[:], func=ACT.Abs_reciprocal_sqrt)
+
         x_sb = keep.tile([P, MAPS, BLOCKS, CHANNELS], BF16)
         x_rows = inputs.rearrange("b h w c -> b (h w) c")
         for b in range(MAPS):
@@ -80,7 +85,7 @@ def tile_levitattention_pa_kernel(
             )
 
         gain_rows = keep.tile([P, P], BF16)
-        nc.vector.memset(gain_rows[:], 0.0)
+        nc.gpsimd.memset(gain_rows[:], 0.0)
         nc.scalar.dma_start(out=gain_rows[0:TILES, :], in_=bn_scale.rearrange("(i f) -> i f", f=P))
 
         identity = keep.tile([P, P], F32)
@@ -109,14 +114,12 @@ def tile_levitattention_pa_kernel(
                 )
 
         gain_wide = keep.tile([P, P], F32)
-        nc.vector.tensor_copy(out=gain_wide[:], in_=gain_rows[:])
+        nc.gpsimd.tensor_copy(out=gain_wide[:], in_=gain_rows[:])
         gain_flipped = psum.tile([P, P], F32, tag="bank", bufs=8)
         nc.tensor.transpose(gain_flipped[:], gain_wide[:], identity[:])
         gain_pair = keep.tile([P, TILES, 2], F32)
-        nc.vector.tensor_copy(out=gain_pair[:, :, 0], in_=gain_flipped[:, 0:TILES])
-        nc.vector.tensor_scalar(
-            out=gain_pair[:, :, 1], in0=gain_flipped[:, 0:TILES], scalar1=-1.0, scalar2=0.0, op0=ALU.mult, op1=ALU.add
-        )
+        nc.scalar.activation(out=gain_pair[:, :, 0], in_=gain_flipped[:, 0:TILES], func=ACT.Copy, scale=1.0)
+        nc.scalar.activation(out=gain_pair[:, :, 1], in_=gain_flipped[:, 0:TILES], func=ACT.Copy, scale=-1.0)
 
         products = {}
         factors = {}
@@ -189,7 +192,10 @@ def tile_levitattention_pa_kernel(
             if part == 0:
                 results[n] = result.tile([P, MAPS, BLOCKS, len(tiles), DIM], F32, name="head", tag="head")
             nc.scalar.copy(out=results[n][:, 0, :, part, :], in_=flips[i][0][:])
-            nc.vector.tensor_copy(out=results[n][:, 1, :, part, :], in_=flips[i][1][:])
+            if i % 3 == 0:
+                nc.scalar.copy(out=results[n][:, 1, :, part, :], in_=flips[i][1][:])
+            else:
+                nc.vector.tensor_copy(out=results[n][:, 1, :, part, :], in_=flips[i][1][:])
             if part == len(tiles) - 1:
                 nc.sync.dma_start(
                     out=dest.rearrange("b (p t) e -> p b (t e)", t=BLOCKS),

@@ -25,6 +25,7 @@ BLOCKS = PIXELS // P
 TILES = COLUMNS // P
 BN_EPS = 1e-5
 STATS = 6
+LAST = 3
 
 FLOPS = 2 * MAPS * PIXELS * CHANNELS * COLUMNS
 
@@ -172,10 +173,16 @@ def tile_levitattention_pa_kernel(
         def normalise(i):
             normalised = normal.tile([P, MAPS, PIXELS], F32)
             for b in range(MAPS):
-                nc.scalar.activation(
-                    out=normalised[:, b, :], in_=products[i][b][:], func=ACT.Identity,
-                    scale=factors[i][:, 2:3], bias=factors[i][:, 1:2],
-                )
+                if b == 1 and i >= TILES - LAST:
+                    nc.vector.tensor_scalar(
+                        out=normalised[:, b, :], in0=products[i][b][:],
+                        scalar1=factors[i][:, 2:3], scalar2=factors[i][:, 1:2], op0=ALU.mult, op1=ALU.add,
+                    )
+                else:
+                    nc.scalar.activation(
+                        out=normalised[:, b, :], in_=products[i][b][:], func=ACT.Identity,
+                        scale=factors[i][:, 2:3], bias=factors[i][:, 1:2],
+                    )
             normals[i] = normalised
 
         def flip(i):
@@ -192,7 +199,7 @@ def tile_levitattention_pa_kernel(
             if part == 0:
                 results[n] = result.tile([P, MAPS, BLOCKS, len(tiles), DIM], F32, name="head", tag="head")
             nc.scalar.copy(out=results[n][:, 0, :, part, :], in_=flips[i][0][:])
-            if i % 3 == 0:
+            if i % 3 == 0 and i < TILES - LAST:
                 nc.scalar.copy(out=results[n][:, 1, :, part, :], in_=flips[i][1][:])
             else:
                 nc.vector.tensor_copy(out=results[n][:, 1, :, part, :], in_=flips[i][1][:])

@@ -120,7 +120,8 @@ def tile_levitattention_pa_kernel(
         nc.tensor.transpose(gain_flipped[:], gain_wide[:], identity[:])
         gain_pair = keep.tile([P, TILES, 2], F32)
         nc.scalar.activation(out=gain_pair[:, :, 0], in_=gain_flipped[:, 0:TILES], func=ACT.Copy, scale=1.0)
-        nc.scalar.activation(out=gain_pair[:, :, 1], in_=gain_flipped[:, 0:TILES], func=ACT.Copy, scale=-1.0)
+        minus_gain = keep.tile([P, TILES], F32)
+        nc.scalar.activation(out=minus_gain[:], in_=gain_flipped[:, 0:TILES], func=ACT.Copy, scale=-1.0)
 
         products = {}
         factors = {}
@@ -156,17 +157,17 @@ def tile_levitattention_pa_kernel(
 
         def chain(i):
             c = work[i][0]
-            factor = small.tile([P, 4], F32)
+            nc.gpsimd.tensor_scalar(
+                out=gain_pair[:, c, 1:2], in0=means[i][:, 0:1], scalar1=minus_gain[:, c : c + 1], scalar2=0.0,
+                op0=ALU.mult, op1=ALU.add,
+            )
+            root = small.tile([P, 1], F32)
             nc.scalar.activation(
-                out=factor[:, 0:1], in_=means[i][:, 1:2], func=ACT.Abs_reciprocal_sqrt, bias=BN_EPS, scale=1.0
+                out=root[:], in_=means[i][:, 1:2], func=ACT.Abs_reciprocal_sqrt, bias=BN_EPS, scale=1.0
             )
+            factor = small.tile([P, 2], F32)
             nc.gpsimd.tensor_scalar(
-                out=factor[:, 2:4], in0=gain_pair[:, c, :], scalar1=factor[:, 0:1], scalar2=0.0,
-                op0=ALU.mult, op1=ALU.add,
-            )
-            nc.gpsimd.tensor_scalar(
-                out=factor[:, 1:2], in0=means[i][:, 0:1], scalar1=factor[:, 3:4], scalar2=0.0,
-                op0=ALU.mult, op1=ALU.add,
+                out=factor[:], in0=gain_pair[:, c, :], scalar1=root[:], scalar2=0.0, op0=ALU.mult, op1=ALU.add
             )
             factors[i] = factor
 
@@ -176,12 +177,12 @@ def tile_levitattention_pa_kernel(
                 if b == 1 and i >= TILES - LAST:
                     nc.vector.tensor_scalar(
                         out=normalised[:, b, :], in0=products[i][b][:],
-                        scalar1=factors[i][:, 2:3], scalar2=factors[i][:, 1:2], op0=ALU.mult, op1=ALU.add,
+                        scalar1=factors[i][:, 0:1], scalar2=factors[i][:, 1:2], op0=ALU.mult, op1=ALU.add,
                     )
                 else:
                     nc.scalar.activation(
                         out=normalised[:, b, :], in_=products[i][b][:], func=ACT.Identity,
-                        scale=factors[i][:, 2:3], bias=factors[i][:, 1:2],
+                        scale=factors[i][:, 0:1], bias=factors[i][:, 1:2],
                     )
             normals[i] = normalised
 

@@ -200,7 +200,7 @@ def tile_levitattention_pa_kernel(
             if part == 0:
                 results[n] = result.tile([P, MAPS, BLOCKS, len(tiles), DIM], F32, name="head", tag="head")
             nc.scalar.copy(out=results[n][:, 0, :, part, :], in_=flips[i][0][:])
-            if i % 3 == 0 and i < TILES - LAST:
+            if i % 3 == 2 and i < TILES - LAST:
                 nc.scalar.copy(out=results[n][:, 1, :, part, :], in_=flips[i][1][:])
             else:
                 nc.vector.tensor_copy(out=results[n][:, 1, :, part, :], in_=flips[i][1][:])

@@ -25,7 +25,7 @@ BLOCKS = PIXELS // P
 TILES = COLUMNS // P
 BN_EPS = 1e-5
 STATS = 6
-LAST = 3
+LAG = 5
 
 FLOPS = 2 * MAPS * PIXELS * CHANNELS * COLUMNS
 
@@ -50,6 +50,7 @@ def tile_levitattention_pa_kernel(
     with ExitStack() as ctx:
         keep = ctx.enter_context(tc.tile_pool(name="keep", bufs=1))
         small = ctx.enter_context(tc.tile_pool(name="small", bufs=6))
+        raws = ctx.enter_context(tc.tile_pool(name="raws", bufs=5))
         normal = ctx.enter_context(tc.tile_pool(name="normal", bufs=4))
         result = ctx.enter_context(tc.tile_pool(name="result", bufs=4))
         psum = ctx.enter_context(tc.psum_pool(name="psum", bufs=1))
@@ -124,11 +125,18 @@ def tile_levitattention_pa_kernel(
         nc.scalar.activation(out=minus_gain[:], in_=gain_flipped[:, 0:TILES], func=ACT.Copy, scale=-1.0)
 
         products = {}
-        factors = {}
+        partials = {}
         means = {}
+        roots = {}
+        factors = {}
+        raw_copies = {}
         normals = {}
         flips = {}
         results = {}
+
+        def pair_columns(m):
+            first, second = work[2 * m][0], work[2 * m + 1][0]
+            return slice(first, second + 1, second - first)
 
         def project(i):
             c = work[i][0]
@@ -146,45 +154,65 @@ def tile_levitattention_pa_kernel(
                 )
                 products[i].append(product)
 
-        def statistics(i):
-            c = work[i][0]
-            partial = small.tile([P, MAPS, STATS], F32)
-            for b in range(MAPS):
-                nc.vector.bn_stats(out=partial[:, b, :], in_=products[i][b][:])
-            mean_var = small.tile([P, 2], F32)
-            nc.vector.bn_aggr(out=mean_var[:], in_=partial[:].rearrange("p b s -> p (b s)"))
-            means[i] = mean_var
+        def statistics(i, b):
+            if b == 0:
+                partials[i] = small.tile([P, MAPS, STATS], F32, name="partial")
+            nc.vector.bn_stats(out=partials[i][:, b, :], in_=products[i][b][:])
 
-        def chain(i):
-            c = work[i][0]
-            nc.gpsimd.tensor_scalar(
-                out=gain_pair[:, c, 1:2], in0=means[i][:, 0:1], scalar1=minus_gain[:, c : c + 1], scalar2=0.0,
-                op0=ALU.mult, op1=ALU.add,
-            )
-            root = small.tile([P, 1], F32)
+        def aggregate(i):
+            m, half = divmod(i, 2)
+            if half == 0:
+                means[m] = small.tile([P, 2, 2], F32, name="mean_var")
+            nc.vector.bn_aggr(out=means[m][:, half, :], in_=partials[i][:].rearrange("p b s -> p (b s)"))
+
+        def root(m):
+            roots[m] = small.tile([P, 2], F32, name="root")
             nc.scalar.activation(
-                out=root[:], in_=means[i][:, 1:2], func=ACT.Abs_reciprocal_sqrt, bias=BN_EPS, scale=1.0
+                out=roots[m][:], in_=means[m][:, :, 1], func=ACT.Abs_reciprocal_sqrt, bias=BN_EPS, scale=1.0
             )
-            factor = small.tile([P, 2], F32)
-            nc.gpsimd.tensor_scalar(
-                out=factor[:], in0=gain_pair[:, c, :], scalar1=root[:], scalar2=0.0, op0=ALU.mult, op1=ALU.add
+
+        def factor(m):
+            columns = pair_columns(m)
+            nc.gpsimd.tensor_tensor(
+                out=gain_pair[:, columns, 1], in0=means[m][:, :, 0], in1=minus_gain[:, columns], op=ALU.mult
             )
-            factors[i] = factor
+            factors[m] = small.tile([P, 2, 2], F32, name="factor")
+            nc.gpsimd.tensor_tensor(
+                out=factors[m][:], in0=gain_pair[:, columns, :],
+                in1=roots[m][:].unsqueeze(2).to_broadcast([P, 2, 2]), op=ALU.mult,
+            )
+
+        def waits(i, b):
+            return i >= TILES - 2 or (i % 2 == 1 and b == 1)
+
+        def copy_raw(i, b):
+            if b == 0:
+                raw_copies[i] = raws.tile([P, MAPS, PIXELS], F32, name="raw")
+            nc.scalar.copy(out=raw_copies[i][:, b, :], in_=products[i][b][:])
 
         def normalise(i):
-            normalised = normal.tile([P, MAPS, PIXELS], F32)
-            for b in range(MAPS):
-                if b == 1 and i >= TILES - LAST:
-                    nc.vector.tensor_scalar(
-                        out=normalised[:, b, :], in0=products[i][b][:],
-                        scalar1=factors[i][:, 0:1], scalar2=factors[i][:, 1:2], op0=ALU.mult, op1=ALU.add,
-                    )
-                else:
-                    nc.scalar.activation(
-                        out=normalised[:, b, :], in_=products[i][b][:], func=ACT.Identity,
-                        scale=factors[i][:, 0:1], bias=factors[i][:, 1:2],
-                    )
-            normals[i] = normalised
+            m, half = divmod(i, 2)
+            normals[i] = normal.tile([P, MAPS, PIXELS], F32, name="normalised")
+            maps = [b for b in range(MAPS) if not waits(i, b)]
+            if maps:
+                nc.gpsimd.tensor_scalar(
+                    out=normals[i][:, 0 : len(maps), :].rearrange("p b n -> p (b n)"),
+                    in0=raw_copies[i][:, 0 : len(maps), :].rearrange("p b n -> p (b n)"),
+                    scalar1=factors[m][:, half, 0:1], scalar2=factors[m][:, half, 1:2], op0=ALU.mult, op1=ALU.add,
+                )
+
+        def normalise_bank(i, b):
+            m, half = divmod(i, 2)
+            scale, shift = factors[m][:, half, 0:1], factors[m][:, half, 1:2]
+            if b == 1 and i >= TILES - 2:
+                nc.vector.tensor_scalar(
+                    out=normals[i][:, b, :], in0=products[i][b][:], scalar1=scale, scalar2=shift,
+                    op0=ALU.mult, op1=ALU.add,
+                )
+            else:
+                nc.scalar.activation(
+                    out=normals[i][:, b, :], in_=products[i][b][:], func=ACT.Identity, scale=scale, bias=shift
+                )
 
         def flip(i):
             flips[i] = []
@@ -200,7 +228,7 @@ def tile_levitattention_pa_kernel(
             if part == 0:
                 results[n] = result.tile([P, MAPS, BLOCKS, len(tiles), DIM], F32, name="head", tag="head")
             nc.scalar.copy(out=results[n][:, 0, :, part, :], in_=flips[i][0][:])
-            if i % 3 == 2 and i < TILES - LAST:
+            if TILES - 2 <= i + LAG < TILES:
                 nc.scalar.copy(out=results[n][:, 1, :, part, :], in_=flips[i][1][:])
             else:
                 nc.vector.tensor_copy(out=results[n][:, 1, :, part, :], in_=flips[i][1][:])
@@ -210,16 +238,34 @@ def tile_levitattention_pa_kernel(
                     in_=results[n][:].rearrange("p b t g d -> p b (t g d)"),
                 )
 
-        for step in range(-1, TILES + 3):
-            if 0 <= step - 2 < TILES:
-                normalise(step - 2)
+        for step in range(-1, TILES + LAG):
             if 0 <= step + 1 < TILES:
                 project(step + 1)
-            if 0 <= step - 3 < TILES:
-                store(step - 3)
             if 0 <= step < TILES:
-                chain(step)
-            if 0 <= step - 2 < TILES:
-                flip(step - 2)
-            if 0 <= step + 1 < TILES:
-                statistics(step + 1)
+                statistics(step, 0)
+            if 0 <= step - 1 < TILES - 1:
+                aggregate(step - 1)
+            if 0 <= step < TILES:
+                statistics(step, 1)
+            if step == TILES - 1:
+                aggregate(step)
+            if 0 <= step - LAG < TILES:
+                store(step - LAG)
+            if 0 <= step < TILES and not waits(step, 0):
+                copy_raw(step, 0)
+            if step % 2 == 0 and 0 <= step - 2 < TILES:
+                root(step // 2 - 1)
+                factor(step // 2 - 1)
+            if 0 <= step < TILES and not waits(step, 1):
+                copy_raw(step, 1)
+            if 0 <= step - 2 < TILES - 2:
+                normalise(step - 2)
+            if step % 2 == 1 and 0 <= step - 2 < TILES - 2:
+                normalise_bank(step - 2, 1)
+            if step == TILES:
+                for i in (TILES - 2, TILES - 1):
+                    normalise(i)
+                    for b in range(MAPS):
+                        normalise_bank(i, b)
+            if 0 <= step - LAG + 1 < TILES:
+                flip(step - LAG + 1)

@@ -25,7 +25,8 @@ BLOCKS = PIXELS // P
 TILES = COLUMNS // P
 BN_EPS = 1e-5
 STATS = 6
-LAG = 5
+LAST = 1
+LAG = 4
 
 FLOPS = 2 * MAPS * PIXELS * CHANNELS * COLUMNS
 
@@ -119,24 +120,19 @@ def tile_levitattention_pa_kernel(
         nc.gpsimd.tensor_copy(out=gain_wide[:], in_=gain_rows[:])
         gain_flipped = psum.tile([P, P], F32, tag="bank", bufs=8)
         nc.tensor.transpose(gain_flipped[:], gain_wide[:], identity[:])
-        gain_pair = keep.tile([P, TILES, 2], F32)
-        nc.scalar.activation(out=gain_pair[:, :, 0], in_=gain_flipped[:, 0:TILES], func=ACT.Copy, scale=1.0)
         minus_gain = keep.tile([P, TILES], F32)
         nc.scalar.activation(out=minus_gain[:], in_=gain_flipped[:, 0:TILES], func=ACT.Copy, scale=-1.0)
+        moments = keep.tile([P, TILES, 4], F32)
+        nc.gpsimd.memset(moments[:], -1.0)
 
         products = {}
         partials = {}
-        means = {}
         roots = {}
         factors = {}
         raw_copies = {}
         normals = {}
         flips = {}
         results = {}
-
-        def pair_columns(m):
-            first, second = work[2 * m][0], work[2 * m + 1][0]
-            return slice(first, second + 1, second - first)
 
         def project(i):
             c = work[i][0]
@@ -160,30 +156,25 @@ def tile_levitattention_pa_kernel(
             nc.vector.bn_stats(out=partials[i][:, b, :], in_=products[i][b][:])
 
         def aggregate(i):
-            m, half = divmod(i, 2)
-            if half == 0:
-                means[m] = small.tile([P, 2, 2], F32, name="mean_var")
-            nc.vector.bn_aggr(out=means[m][:, half, :], in_=partials[i][:].rearrange("p b s -> p (b s)"))
+            nc.vector.bn_aggr(out=moments[:, i, 1:3], in_=partials[i][:].rearrange("p b s -> p (b s)"))
 
-        def root(m):
-            roots[m] = small.tile([P, 2], F32, name="root")
+        def root(i):
+            roots[i] = small.tile([P, 1], F32, name="root")
             nc.scalar.activation(
-                out=roots[m][:], in_=means[m][:, :, 1], func=ACT.Abs_reciprocal_sqrt, bias=BN_EPS, scale=1.0
+                out=roots[i][:], in_=moments[:, i, 2:3], func=ACT.Abs_reciprocal_sqrt, bias=BN_EPS, scale=1.0
             )
 
-        def factor(m):
-            columns = pair_columns(m)
-            nc.gpsimd.tensor_tensor(
-                out=gain_pair[:, columns, 1], in0=means[m][:, :, 0], in1=minus_gain[:, columns], op=ALU.mult
-            )
-            factors[m] = small.tile([P, 2, 2], F32, name="factor")
-            nc.gpsimd.tensor_tensor(
-                out=factors[m][:], in0=gain_pair[:, columns, :],
-                in1=roots[m][:].unsqueeze(2).to_broadcast([P, 2, 2]), op=ALU.mult,
+        def factor(i):
+            c = work[i][0]
+            factors[i] = small.tile([P, 2], F32, name="factor")
+            engine = nc.vector if i == TILES - 1 else nc.gpsimd
+            engine.tensor_scalar(
+                out=factors[i][:], in0=moments[:, i, 0:2], scalar1=minus_gain[:, c : c + 1], scalar2=roots[i][:],
+                op0=ALU.mult, op1=ALU.mult,
             )
 
         def waits(i, b):
-            return i >= TILES - 2 or (i % 2 == 1 and b == 1)
+            return i >= TILES - LAST or (i % 2 == 1 and b == 1)
 
         def copy_raw(i, b):
             if b == 0:
@@ -191,20 +182,18 @@ def tile_levitattention_pa_kernel(
             nc.scalar.copy(out=raw_copies[i][:, b, :], in_=products[i][b][:])
 
         def normalise(i):
-            m, half = divmod(i, 2)
             normals[i] = normal.tile([P, MAPS, PIXELS], F32, name="normalised")
             maps = [b for b in range(MAPS) if not waits(i, b)]
             if maps:
                 nc.gpsimd.tensor_scalar(
                     out=normals[i][:, 0 : len(maps), :].rearrange("p b n -> p (b n)"),
                     in0=raw_copies[i][:, 0 : len(maps), :].rearrange("p b n -> p (b n)"),
-                    scalar1=factors[m][:, half, 0:1], scalar2=factors[m][:, half, 1:2], op0=ALU.mult, op1=ALU.add,
+                    scalar1=factors[i][:, 0:1], scalar2=factors[i][:, 1:2], op0=ALU.mult, op1=ALU.add,
                 )
 
         def normalise_bank(i, b):
-            m, half = divmod(i, 2)
-            scale, shift = factors[m][:, half, 0:1], factors[m][:, half, 1:2]
-            if b == 1 and i >= TILES - 2:
+            scale, shift = factors[i][:, 0:1], factors[i][:, 1:2]
+            if b == 1 and i >= TILES - LAST:
                 nc.vector.tensor_scalar(
                     out=normals[i][:, b, :], in0=products[i][b][:], scalar1=scale, scalar2=shift,
                     op0=ALU.mult, op1=ALU.add,
@@ -228,7 +217,7 @@ def tile_levitattention_pa_kernel(
             if part == 0:
                 results[n] = result.tile([P, MAPS, BLOCKS, len(tiles), DIM], F32, name="head", tag="head")
             nc.scalar.copy(out=results[n][:, 0, :, part, :], in_=flips[i][0][:])
-            if TILES - 2 <= i + LAG < TILES:
+            if TILES - LAST <= i + LAG < TILES:
                 nc.scalar.copy(out=results[n][:, 1, :, part, :], in_=flips[i][1][:])
             else:
                 nc.vector.tensor_copy(out=results[n][:, 1, :, part, :], in_=flips[i][1][:])
@@ -243,29 +232,24 @@ def tile_levitattention_pa_kernel(
                 project(step + 1)
             if 0 <= step < TILES:
                 statistics(step, 0)
-            if 0 <= step - 1 < TILES - 1:
+            if 0 <= step - 1 < TILES:
                 aggregate(step - 1)
             if 0 <= step < TILES:
                 statistics(step, 1)
-            if step == TILES - 1:
-                aggregate(step)
-            if 0 <= step - LAG < TILES:
-                store(step - LAG)
+            if 0 <= step - 1 < TILES:
+                root(step - 1)
+                factor(step - 1)
+                normalise(step - 1)
             if 0 <= step < TILES and not waits(step, 0):
                 copy_raw(step, 0)
-            if step % 2 == 0 and 0 <= step - 2 < TILES:
-                root(step // 2 - 1)
-                factor(step // 2 - 1)
+            if 0 <= step - LAG < TILES:
+                store(step - LAG)
             if 0 <= step < TILES and not waits(step, 1):
                 copy_raw(step, 1)
-            if 0 <= step - 2 < TILES - 2:
-                normalise(step - 2)
-            if step % 2 == 1 and 0 <= step - 2 < TILES - 2:
+            if step % 2 == 1 and 0 <= step - 2 < TILES - LAST:
                 normalise_bank(step - 2, 1)
-            if step == TILES:
-                for i in (TILES - 2, TILES - 1):
-                    normalise(i)
-                    for b in range(MAPS):
-                        normalise_bank(i, b)
+            if TILES - LAST <= step - 1 < TILES:
+                for b in range(MAPS):
+                    normalise_bank(step - 1, b)
             if 0 <= step - LAG + 1 < TILES:
                 flip(step - LAG + 1)

@@ -25,7 +25,9 @@ BLOCKS = PIXELS // P
 TILES = COLUMNS // P
 BN_EPS = 1e-5
 STATS = 6
+IDLE_PASSES = 15
 LAST = 1
+NEAR_END = 6
 LAG = 4
 
 FLOPS = 2 * MAPS * PIXELS * CHANNELS * COLUMNS
@@ -56,6 +58,12 @@ def tile_levitattention_pa_kernel(
         result = ctx.enter_context(tc.tile_pool(name="result", bufs=4))
         psum = ctx.enter_context(tc.psum_pool(name="psum", bufs=1))
         ctx.enter_context(tc.manual_schedule())
+
+        zeros = keep.tile([P, P], BF16)
+        nc.gpsimd.memset(zeros[:], 0.0)
+        idle = psum.tile([P, P], F32, tag="bank", bufs=8)
+        for n in range(IDLE_PASSES):
+            nc.tensor.matmul(idle[:], lhsT=zeros[:], rhs=zeros[:], start=True, stop=True)
 
         one = keep.tile([P, 1], F32)
         nc.gpsimd.memset(one[:], 1.0)
@@ -106,10 +114,7 @@ def tile_levitattention_pa_kernel(
                         nc.tensor.transpose(flipped[:, j, u, :], words[:, u : CHANNELS // 2 : 2], identity[:])
                 pixels = slice(2 * pair * P, 2 * (pair + 1) * P)
                 side_by_side = grouped[:, pixels, :].bitcast(F32).rearrange("p (j r) u -> p j r u", j=2)
-                if pair == 0:
-                    nc.vector.tensor_copy(out=side_by_side, in_=flipped[:].rearrange("p j u r -> p j r u"))
-                else:
-                    nc.scalar.copy(out=side_by_side, in_=flipped[:].rearrange("p j u r -> p j r u"))
+                nc.scalar.copy(out=side_by_side, in_=flipped[:].rearrange("p j u r -> p j r u"))
                 nc.vector.quantize_mx(
                     out=x_codes[:, b, pixels].bitcast(FP8X4),
                     scales=x_plane[:, b, pixels],
@@ -174,7 +179,7 @@ def tile_levitattention_pa_kernel(
             )
 
         def waits(i, b):
-            return i >= TILES - LAST or (i % 2 == 1 and b == 1)
+            return i >= TILES - LAST or (b == 1 and (i % 2 == 1 or i >= TILES - NEAR_END))
 
         def copy_raw(i, b):
             if b == 0:
@@ -211,21 +216,18 @@ def tile_levitattention_pa_kernel(
                     nc.tensor.transpose(flipped[:, t, :], normals[i][:, b, t * P : (t + 1) * P], identity[:])
                 flips[i].append(flipped)
 
-        def store(i):
+        def store(i, b):
             c, n, part = work[i]
             dest, tiles = stores[n]
-            if part == 0:
+            if part == 0 and b == 0:
                 results[n] = result.tile([P, MAPS, BLOCKS, len(tiles), DIM], F32, name="head", tag="head")
-            nc.scalar.copy(out=results[n][:, 0, :, part, :], in_=flips[i][0][:])
-            if TILES - LAST <= i + LAG < TILES:
-                nc.scalar.copy(out=results[n][:, 1, :, part, :], in_=flips[i][1][:])
+            if b == 0:
+                nc.scalar.copy(out=results[n][:, b, :, part, :], in_=flips[i][b][:])
             else:
-                nc.vector.tensor_copy(out=results[n][:, 1, :, part, :], in_=flips[i][1][:])
+                nc.vector.tensor_copy(out=results[n][:, b, :, part, :], in_=flips[i][b][:])
             if part == len(tiles) - 1:
-                nc.sync.dma_start(
-                    out=dest.rearrange("b (p t) e -> p b (t e)", t=BLOCKS),
-                    in_=results[n][:].rearrange("p b t g d -> p b (t g d)"),
-                )
+                rows = dest.rearrange("b (p t) e -> p b (t e)", t=BLOCKS)
+                nc.sync.dma_start(out=rows[:, b, :], in_=results[n][:, b].rearrange("p t g d -> p (t g d)"))
 
         for step in range(-1, TILES + LAG):
             if 0 <= step + 1 < TILES:
@@ -236,20 +238,22 @@ def tile_levitattention_pa_kernel(
                 aggregate(step - 1)
             if 0 <= step < TILES:
                 statistics(step, 1)
+            if 0 <= step - LAG < TILES:
+                store(step - LAG, 0)
             if 0 <= step - 1 < TILES:
                 root(step - 1)
                 factor(step - 1)
                 normalise(step - 1)
             if 0 <= step < TILES and not waits(step, 0):
                 copy_raw(step, 0)
-            if 0 <= step - LAG < TILES:
-                store(step - LAG)
             if 0 <= step < TILES and not waits(step, 1):
                 copy_raw(step, 1)
-            if step % 2 == 1 and 0 <= step - 2 < TILES - LAST:
+            if 0 <= step - 2 < TILES - LAST and waits(step - 2, 1):
                 normalise_bank(step - 2, 1)
             if TILES - LAST <= step - 1 < TILES:
                 for b in range(MAPS):
                     normalise_bank(step - 1, b)
+            if 0 <= step - LAG < TILES:
+                store(step - LAG, 1)
             if 0 <= step - LAG + 1 < TILES:
                 flip(step - LAG + 1)

@@ -106,6 +106,7 @@ def tile_levitattention_pa_kernel(
         x_plane = keep.tile([P, MAPS, PIXELS], U8, align_bytes=64)
         for b in range(MAPS):
             grouped = keep.tile([P, PIXELS, PACK], BF16, align_bytes=64, name="grouped%d" % b)
+            busy_rows = grouped[:, 0:P, :].rearrange("p r t -> p (r t)")
             for pair in range(BLOCKS // 2):
                 flipped = psum.tile([P, 2, 2, P], F32, tag="bank", bufs=8)
                 for j in range(2):
@@ -229,6 +230,10 @@ def tile_levitattention_pa_kernel(
                 rows = dest.rearrange("b (p t) e -> p b (t e)", t=BLOCKS)
                 nc.sync.dma_start(out=rows[:, b, :], in_=results[n][:, b].rearrange("p t g d -> p (t g d)"))
 
+        def keep_busy():
+            idle = psum.tile([P, PIXELS], F32, tag="bank", bufs=8)
+            nc.tensor.matmul(idle[:], lhsT=zeros[:], rhs=busy_rows, start=True, stop=True)
+
         for step in range(-1, TILES + LAG):
             if 0 <= step + 1 < TILES:
                 project(step + 1)
@@ -256,4 +261,6 @@ def tile_levitattention_pa_kernel(
             if 0 <= step - LAG < TILES:
                 store(step - LAG, 1)
             if 0 <= step - LAG + 1 < TILES:
+                if step >= TILES:
+                    keep_busy()
                 flip(step - LAG + 1)

@@ -27,7 +27,7 @@ BN_EPS = 1e-5
 STATS = 6
 IDLE_PASSES = 15
 LAST = 1
-NEAR_END = 6
+NEAR_END = 4
 LAG = 4
 
 FLOPS = 2 * MAPS * PIXELS * CHANNELS * COLUMNS
@@ -53,9 +53,9 @@ def tile_levitattention_pa_kernel(
     with ExitStack() as ctx:
         keep = ctx.enter_context(tc.tile_pool(name="keep", bufs=1))
         small = ctx.enter_context(tc.tile_pool(name="small", bufs=6))
-        raws = ctx.enter_context(tc.tile_pool(name="raws", bufs=5))
-        normal = ctx.enter_context(tc.tile_pool(name="normal", bufs=4))
-        result = ctx.enter_context(tc.tile_pool(name="result", bufs=4))
+        raws = ctx.enter_context(tc.tile_pool(name="raws", bufs=6))
+        normal = ctx.enter_context(tc.tile_pool(name="normal", bufs=6))
+        result = ctx.enter_context(tc.tile_pool(name="result", bufs=6))
         psum = ctx.enter_context(tc.psum_pool(name="psum", bufs=1))
         ctx.enter_context(tc.manual_schedule())
 
@@ -180,7 +180,7 @@ def tile_levitattention_pa_kernel(
             )
 
         def waits(i, b):
-            return i >= TILES - LAST or (b == 1 and (i % 2 == 1 or i >= TILES - NEAR_END))
+            return i >= TILES - LAST or (b == 1 and i % 2 == 1)
 
         def copy_raw(i, b):
             if b == 0:
@@ -222,45 +222,62 @@ def tile_levitattention_pa_kernel(
             dest, tiles = stores[n]
             if part == 0 and b == 0:
                 results[n] = result.tile([P, MAPS, BLOCKS, len(tiles), DIM], F32, name="head", tag="head")
-            if b == 0:
-                nc.scalar.copy(out=results[n][:, b, :, part, :], in_=flips[i][b][:])
-            else:
-                nc.vector.tensor_copy(out=results[n][:, b, :, part, :], in_=flips[i][b][:])
-            if part == len(tiles) - 1:
-                rows = dest.rearrange("b (p t) e -> p b (t e)", t=BLOCKS)
-                nc.sync.dma_start(out=rows[:, b, :], in_=results[n][:, b].rearrange("p t g d -> p (t g d)"))
+            rows = dest.rearrange("b (p t) e -> p b t e", t=BLOCKS)
+            pieces = 2 if i == TILES - 1 else 1
+            for piece in range(pieces):
+                blocks = slice(piece * BLOCKS // pieces, (piece + 1) * BLOCKS // pieces)
+                if b == 0:
+                    nc.scalar.copy(out=results[n][:, b, blocks, part, :], in_=flips[i][b][:, blocks, :])
+                else:
+                    nc.vector.tensor_copy(out=results[n][:, b, blocks, part, :], in_=flips[i][b][:, blocks, :])
+                if part == len(tiles) - 1:
+                    nc.sync.dma_start(
+                        out=rows[:, b, blocks, :],
+                        in_=results[n][:, b, blocks].rearrange("p t g d -> p t (g d)"),
+                    )
 
         def keep_busy():
             idle = psum.tile([P, PIXELS], F32, tag="bank", bufs=8)
             nc.tensor.matmul(idle[:], lhsT=zeros[:], rhs=busy_rows, start=True, stop=True)
 
+        copies = {}
+        for i in range(TILES):
+            copies.setdefault(i + (LAG if i < TILES - NEAR_END else LAG - 1), []).append(i)
         for step in range(-1, TILES + LAG):
             if 0 <= step + 1 < TILES:
                 project(step + 1)
             if 0 <= step < TILES:
                 statistics(step, 0)
-            if 0 <= step - 1 < TILES:
+            if 0 <= step - 1 < TILES - 1:
                 aggregate(step - 1)
             if 0 <= step < TILES:
                 statistics(step, 1)
-            if 0 <= step - LAG < TILES:
-                store(step - LAG, 0)
-            if 0 <= step - 1 < TILES:
+            if 0 <= step - 1 < TILES - 1:
                 root(step - 1)
                 factor(step - 1)
                 normalise(step - 1)
             if 0 <= step < TILES and not waits(step, 0):
                 copy_raw(step, 0)
+            for i in copies.get(step, []):
+                store(i, 0)
             if 0 <= step < TILES and not waits(step, 1):
                 copy_raw(step, 1)
+            ready = copies.get(step, [])
+            if step == TILES - 1:
+                store(ready[0], 1)
+                aggregate(step)
+                root(step)
+                ready = ready[1:]
             if 0 <= step - 2 < TILES - LAST and waits(step - 2, 1):
                 normalise_bank(step - 2, 1)
-            if TILES - LAST <= step - 1 < TILES:
+            if step == TILES:
+                factor(step - 1)
+                normalise(step - 1)
                 for b in range(MAPS):
                     normalise_bank(step - 1, b)
-            if 0 <= step - LAG < TILES:
-                store(step - LAG, 1)
-            if 0 <= step - LAG + 1 < TILES:
-                if step >= TILES:
+            for i in ready:
+                store(i, 1)
+            for i in copies.get(step + 1, []):
+                if i >= TILES - 3:
                     keep_busy()
-                flip(step - LAG + 1)
+                flip(i)

from contextlib import ExitStack

import concourse.mybir as mybir
from concourse.masks import make_identity

F32 = mybir.dt.float32
BF16 = mybir.dt.bfloat16
I32 = mybir.dt.int32
U32 = mybir.dt.uint32
U8 = mybir.dt.uint8
FP8X4 = mybir.dt.float8_e4m3fn_x4
FP4X4 = mybir.dt.float4_e2m1fn_x4
ALU = mybir.AluOpType
ACT = mybir.ActivationFunctionType

P = 128
PACK = 4
MAPS = 2
PIXELS = 512
CHANNELS = 512
COLUMNS = 4096
HEADS = 8
DIM = 128
BLOCKS = PIXELS // P
TILES = COLUMNS // P
BN_EPS = 1e-5
STATS = 6
IDLE_PASSES = 15
LAST = 1
NEAR_END = 4
LAG = 4

FLOPS = 2 * MAPS * PIXELS * CHANNELS * COLUMNS


def tile_levitattention_pa_kernel(
    tc, inputs, w_qkv_words, w_qkv_scales, bn_scale, out_0, out_1, out_2
):
    nc = tc.nc

    stores = []
    for h in range(HEADS):
        stores.append((out_2[:, h], [2 * HEADS + h, 3 * HEADS + h]))
    for h in range(HEADS):
        stores.append((out_0[:, h], [h]))
    for h in range(HEADS):
        stores.append((out_1[:, h], [HEADS + h]))
    work = []
    for n, (dest, tiles) in enumerate(stores):
        for part, c in enumerate(tiles):
            work.append((c, n, part))

    with ExitStack() as ctx:
        keep = ctx.enter_context(tc.tile_pool(name="keep", bufs=1))
        small = ctx.enter_context(tc.tile_pool(name="small", bufs=6))
        raws = ctx.enter_context(tc.tile_pool(name="raws", bufs=6))
        normal = ctx.enter_context(tc.tile_pool(name="normal", bufs=6))
        result = ctx.enter_context(tc.tile_pool(name="result", bufs=6))
        psum = ctx.enter_context(tc.psum_pool(name="psum", bufs=1))
        ctx.enter_context(tc.manual_schedule())

        zeros = keep.tile([P, P], BF16)
        nc.gpsimd.memset(zeros[:], 0.0)
        idle = psum.tile([P, P], F32, tag="bank", bufs=8)
        for n in range(IDLE_PASSES):
            nc.tensor.matmul(idle[:], lhsT=zeros[:], rhs=zeros[:], start=True, stop=True)

        one = keep.tile([P, 1], F32)
        nc.gpsimd.memset(one[:], 1.0)
        warm = keep.tile([P, 1], F32)
        nc.scalar.activation(out=warm[:], in_=one[:], func=ACT.Abs_reciprocal_sqrt)

        x_sb = keep.tile([P, MAPS, BLOCKS, CHANNELS], BF16)
        x_rows = inputs.rearrange("b h w c -> b (h w) c")
        for b in range(MAPS):
            x_map = x_rows[b].rearrange("(p t) c -> p t c", t=BLOCKS)
            for pair in range(BLOCKS // 2):
                nc.sync.dma_start(
                    out=x_sb[:, b, 2 * pair : 2 * pair + 2, :], in_=x_map[:, 2 * pair : 2 * pair + 2, :]
                )

        w_plane = keep.tile([P, COLUMNS], U8, align_bytes=64)
        nc.vector.memset(w_plane[:].bitcast(I32), 0)
        for quadrant in range(4):
            nc.sync.dma_start(
                out=w_plane[32 * quadrant : 32 * quadrant + 4, :].bitcast(I32),
                in_=w_qkv_scales[0, 4 * quadrant : 4 * quadrant + 4, :].bitcast(I32),
            )

        w_words = keep.tile([P, 2 * COLUMNS], U8, align_bytes=64)
        quarter = 2 * COLUMNS // 4
        for j in (2, 3, 0, 1):
            nc.sync.dma_start(
                out=w_words[:, j * quarter : (j + 1) * quarter].bitcast(I32),
                in_=w_qkv_words[0, :, j * quarter : (j + 1) * quarter].bitcast(I32),
            )

        gain_rows = keep.tile([P, P], BF16)
        nc.gpsimd.memset(gain_rows[:], 0.0)
        nc.scalar.dma_start(out=gain_rows[0:TILES, :], in_=bn_scale.rearrange("(i f) -> i f", f=P))

        identity = keep.tile([P, P], F32)
        make_identity(nc, identity[:])

        x_codes = keep.tile([P, MAPS, PIXELS], U32, align_bytes=64)
        x_plane = keep.tile([P, MAPS, PIXELS], U8, align_bytes=64)
        for b in range(MAPS):
            grouped = keep.tile([P, PIXELS, PACK], BF16, align_bytes=64, name="grouped%d" % b)
            busy_rows = grouped[:, 0:P, :].rearrange("p r t -> p (r t)")
            for pair in range(BLOCKS // 2):
                flipped = psum.tile([P, 2, 2, P], F32, tag="bank", bufs=8)
                for j in range(2):
                    words = x_sb[:, b, 2 * pair + j, :].bitcast(F32)
                    for u in range(2):
                        nc.tensor.transpose(flipped[:, j, u, :], words[:, u : CHANNELS // 2 : 2], identity[:])
                pixels = slice(2 * pair * P, 2 * (pair + 1) * P)
                side_by_side = grouped[:, pixels, :].bitcast(F32).rearrange("p (j r) u -> p j r u", j=2)
                nc.scalar.copy(out=side_by_side, in_=flipped[:].rearrange("p j u r -> p j r u"))
                nc.vector.quantize_mx(
                    out=x_codes[:, b, pixels].bitcast(FP8X4),
                    scales=x_plane[:, b, pixels],
                    in_=grouped[:, pixels, :].rearrange("p r t -> p (r t)"),
                )

        gain_wide = keep.tile([P, P], F32)
        nc.gpsimd.tensor_copy(out=gain_wide[:], in_=gain_rows[:])
        gain_flipped = psum.tile([P, P], F32, tag="bank", bufs=8)
        nc.tensor.transpose(gain_flipped[:], gain_wide[:], identity[:])
        minus_gain = keep.tile([P, TILES], F32)
        nc.scalar.activation(out=minus_gain[:], in_=gain_flipped[:, 0:TILES], func=ACT.Copy, scale=-1.0)
        moments = keep.tile([P, TILES, 4], F32)
        nc.gpsimd.memset(moments[:], -1.0)

        products = {}
        partials = {}
        roots = {}
        factors = {}
        raw_copies = {}
        normals = {}
        flips = {}
        results = {}

        def project(i):
            c = work[i][0]
            products[i] = []
            for b in range(MAPS):
                product = psum.tile([P, PIXELS], F32, tag="bank", bufs=8)
                nc.tensor.matmul_mx(
                    out=product[:],
                    lhsT=w_words[:, 2 * c * P : 2 * (c + 1) * P].bitcast(FP4X4),
                    lhsT_scale=w_plane[:, c * P : (c + 1) * P],
                    rhs=x_codes[:, b, :].bitcast(FP8X4),
                    rhs_scale=x_plane[:, b, :],
                    start=True,
                    stop=True,
                )
                products[i].append(product)

        def statistics(i, b):
            if b == 0:
                partials[i] = small.tile([P, MAPS, STATS], F32, name="partial")
            nc.vector.bn_stats(out=partials[i][:, b, :], in_=products[i][b][:])

        def aggregate(i):
            nc.vector.bn_aggr(out=moments[:, i, 1:3], in_=partials[i][:].rearrange("p b s -> p (b s)"))

        def root(i):
            roots[i] = small.tile([P, 1], F32, name="root")
            nc.scalar.activation(
                out=roots[i][:], in_=moments[:, i, 2:3], func=ACT.Abs_reciprocal_sqrt, bias=BN_EPS, scale=1.0
            )

        def factor(i):
            c = work[i][0]
            factors[i] = small.tile([P, 2], F32, name="factor")
            engine = nc.vector if i == TILES - 1 else nc.gpsimd
            engine.tensor_scalar(
                out=factors[i][:], in0=moments[:, i, 0:2], scalar1=minus_gain[:, c : c + 1], scalar2=roots[i][:],
                op0=ALU.mult, op1=ALU.mult,
            )

        def waits(i, b):
            return i >= TILES - LAST or (b == 1 and i % 2 == 1)

        def copy_raw(i, b):
            if b == 0:
                raw_copies[i] = raws.tile([P, MAPS, PIXELS], F32, name="raw")
            nc.scalar.copy(out=raw_copies[i][:, b, :], in_=products[i][b][:])

        def normalise(i):
            normals[i] = normal.tile([P, MAPS, PIXELS], F32, name="normalised")
            maps = [b for b in range(MAPS) if not waits(i, b)]
            if maps:
                nc.gpsimd.tensor_scalar(
                    out=normals[i][:, 0 : len(maps), :].rearrange("p b n -> p (b n)"),
                    in0=raw_copies[i][:, 0 : len(maps), :].rearrange("p b n -> p (b n)"),
                    scalar1=factors[i][:, 0:1], scalar2=factors[i][:, 1:2], op0=ALU.mult, op1=ALU.add,
                )

        def normalise_bank(i, b):
            scale, shift = factors[i][:, 0:1], factors[i][:, 1:2]
            if b == 1 and i >= TILES - LAST:
                nc.vector.tensor_scalar(
                    out=normals[i][:, b, :], in0=products[i][b][:], scalar1=scale, scalar2=shift,
                    op0=ALU.mult, op1=ALU.add,
                )
            else:
                nc.scalar.activation(
                    out=normals[i][:, b, :], in_=products[i][b][:], func=ACT.Identity, scale=scale, bias=shift
                )

        def flip(i):
            flips[i] = []
            for b in range(MAPS):
                flipped = psum.tile([P, BLOCKS, DIM], F32, tag="bank", bufs=8)
                for t in range(BLOCKS):
                    nc.tensor.transpose(flipped[:, t, :], normals[i][:, b, t * P : (t + 1) * P], identity[:])
                flips[i].append(flipped)

        def store(i, b):
            c, n, part = work[i]
            dest, tiles = stores[n]
            if part == 0 and b == 0:
                results[n] = result.tile([P, MAPS, BLOCKS, len(tiles), DIM], F32, name="head", tag="head")
            rows = dest.rearrange("b (p t) e -> p b t e", t=BLOCKS)
            pieces = 2 if i == TILES - 1 else 1
            for piece in range(pieces):
                blocks = slice(piece * BLOCKS // pieces, (piece + 1) * BLOCKS // pieces)
                if b == 0:
                    nc.scalar.copy(out=results[n][:, b, blocks, part, :], in_=flips[i][b][:, blocks, :])
                else:
                    nc.vector.tensor_copy(out=results[n][:, b, blocks, part, :], in_=flips[i][b][:, blocks, :])
                if part == len(tiles) - 1:
                    nc.sync.dma_start(
                        out=rows[:, b, blocks, :],
                        in_=results[n][:, b, blocks].rearrange("p t g d -> p t (g d)"),
                    )

        def keep_busy():
            idle = psum.tile([P, PIXELS], F32, tag="bank", bufs=8)
            nc.tensor.matmul(idle[:], lhsT=zeros[:], rhs=busy_rows, start=True, stop=True)

        copies = {}
        for i in range(TILES):
            copies.setdefault(i + (LAG if i < TILES - NEAR_END else LAG - 1), []).append(i)
        for step in range(-1, TILES + LAG):
            if 0 <= step + 1 < TILES:
                project(step + 1)
            if 0 <= step < TILES:
                statistics(step, 0)
            if 0 <= step - 1 < TILES - 1:
                aggregate(step - 1)
            if 0 <= step < TILES:
                statistics(step, 1)
            if 0 <= step - 1 < TILES - 1:
                root(step - 1)
                factor(step - 1)
                normalise(step - 1)
            if 0 <= step < TILES and not waits(step, 0):
                copy_raw(step, 0)
            for i in copies.get(step, []):
                store(i, 0)
            if 0 <= step < TILES and not waits(step, 1):
                copy_raw(step, 1)
            ready = copies.get(step, [])
            if step == TILES - 1:
                store(ready[0], 1)
                aggregate(step)
                root(step)
                ready = ready[1:]
            if 0 <= step - 2 < TILES - LAST and waits(step - 2, 1):
                normalise_bank(step - 2, 1)
            if step == TILES:
                factor(step - 1)
                normalise(step - 1)
                for b in range(MAPS):
                    normalise_bank(step - 1, b)
            for i in ready:
                store(i, 1)
            for i in copies.get(step + 1, []):
                if i >= TILES - 3:
                    keep_busy()
                flip(i)
